import numpy as np
import ml_dtypes


def mxq(x, axis, fmt="e4m3"):
    dtype, down = {"e4m3": (ml_dtypes.float8_e4m3fn, 7), "e5m2": (ml_dtypes.float8_e5m2, 14)}[fmt]
    v = np.moveaxis(np.asarray(x, np.float32).astype(ml_dtypes.bfloat16).astype(np.float64), axis, -1)
    blocks = v.reshape(v.shape[:-1] + (-1, 32))
    amax = np.abs(blocks).max(-1, keepdims=True)
    byte = np.maximum(np.where(amax > 0, np.frexp(amax)[1] - 1 + 127, 0) - down, 1)
    scale = np.exp2(byte - 127.0)
    codes = (blocks / scale).astype(np.float32).astype(dtype).astype(np.float64)
    return np.moveaxis((codes * scale).reshape(v.shape), -1, axis)


WIDE = False


def mx_kscale(k):
    if not WIDE:
        return np.ones(k)
    levels = np.array([10, -10, 5, -5, 0])
    if k % 512:
        return np.exp2(np.random.permutation(np.resize(levels, k // 32))).repeat(32)
    a = np.empty((k // 512, 16))
    for p in range(k // 512):
        a[p, :8] = np.random.permutation(np.resize(levels, 8))
        for g in range(8):
            far = levels[np.abs(levels - a[p, g]) >= 10]
            a[p, g + 8] = far[np.random.randint(len(far))]
    return np.exp2(a.ravel()).repeat(32)


BF16 = ml_dtypes.bfloat16


def bf(x):
    return np.asarray(x, np.float32).astype(BF16)


def f64(x):
    return np.asarray(x).astype(np.float64)


B, H, W, C, F, K, G, RR = 4, 32, 32, 1024, 256, 3, 16, 4
KK = K * K
P = B * H * W


def draw0():
    s = mx_kscale(C)
    return {"x": bf(np.random.standard_normal((B, H, W, C)) * s),
            "Wi": bf(np.random.standard_normal((C, F)) / np.sqrt(C) / s[:, None]),
            "bi": bf(np.random.standard_normal(F) * 0.3),
            "w_span": bf(np.random.standard_normal((B, H, W, KK * G)) * 0.7)}


def core(x, Wi, bi, w_span):
    xi = ((mxq(f64(x).reshape(P, C), 1, "e4m3") @ mxq(f64(Wi), 0, "e4m3")) + f64(bi)).reshape(B, H, W, F)
    pad = (K - 1) // 2
    xp = np.pad(xi, ((0, 0), (pad, pad), (pad, pad), (0, 0)))
    patches = np.stack([xp[:, i:i + H, j:j + W, :] for i in range(K) for j in range(K)], axis=-2)
    patches = patches.reshape(B, H, W, G, F // G, KK)
    w = f64(w_span).reshape(B, H, W, G, KK)[:, :, :, :, None, :]
    return (w * patches).sum(-1).reshape(B, H, W, F)


def e4m3fn_bytes(y):
    return np.clip(np.asarray(y, np.float64), -448.0, 448.0).astype(np.float32).astype(ml_dtypes.float8_e4m3fn).view(np.uint8)


def e4m3fn_values(b):
    return np.asarray(b, np.uint8).view(ml_dtypes.float8_e4m3fn).astype(np.float64)


def setup_inputs():
    d = draw0()
    x0 = np.asarray(d['x']).astype(np.float64)
    s = (np.max(np.abs(x0), axis=(0, 1, 2), keepdims=True) / 448.0).astype(np.float32)
    out = {}
    for k, v in d.items():
        if k == 'x':
            out['x_bytes'] = e4m3fn_bytes(x0 / s.astype(np.float64))
            out['x_scale'] = s
        else:
            out[k] = v
    return out


def reference(x_bytes, x_scale, Wi, bi, w_span):
    return core(e4m3fn_values(x_bytes) * x_scale.astype(np.float64), Wi, bi, w_span)

@@ -1,0 +1,393 @@
+from contextlib import ExitStack
+
+import concourse.mybir as mybir
+from concourse.masks import make_identity
+
+FLOPS = 2 * 4096 * 1024 * 256 + 2 * 4096 * 256 * 9
+
+F32 = mybir.dt.float32
+BF16 = mybir.dt.bfloat16
+U32 = mybir.dt.uint32
+U8 = mybir.dt.uint8
+FP8 = mybir.dt.float8_e4m3fn
+FP8X4 = mybir.dt.float8_e4m3fn_x4
+MULT = mybir.AluOpType.mult
+ADD = mybir.AluOpType.add
+ACT = mybir.ActivationFunctionType
+
+P = 128
+NV = 32
+C = 1024
+F = 256
+TAPS = 9
+GRP = 144
+ROW3 = 768
+HALF = 1152
+NB = 4
+NCH = NV // 2
+WCOL = 81
+G_JOBS = ((0, 0, 4), (1, 0, 4), (2, 0, 4), (3, 0, 4), (4, 0, 4), (5, 0, 2))
+G_AFTER = (3, 5, 8, 10, 14, 16)
+V_JOBS = (
+    (5, 2, 2), (6, 0, 4), (7, 0, 4), (8, 0, 4), (9, 0, 4), (10, 0, 4), (11, 0, 4), (12, 0, 4),
+    (13, 0, 2), (13, 2, 2), (14, 0, 4), (15, 0, 4),
+)
+V_SUM = ((7, 0, 4), (9, 0, 4), (11, 0, 4), (13, 2, 2), (14, 0, 4), (15, 0, 4))
+
+
+def pieces(h):
+    res = []
+    f = HALF * h
+    end = HALF * (h + 1)
+    while f < end:
+        nxt = min(end, (f // GRP + 1) * GRP, (f // ROW3 + 1) * ROW3)
+        lo = f
+        if lo % TAPS:
+            e = min(nxt, lo + TAPS - lo % TAPS)
+            res.append((lo, e, False))
+            lo = e
+        body = nxt - (nxt - lo) % TAPS
+        if body > lo:
+            res.append((lo, body, True))
+        if nxt > body:
+            res.append((body, nxt, False))
+        f = nxt
+    return res
+
+
+def tile_involution2d_pa_kernel(tc, x_bytes, x_scale, Wi, bi, w_span, out):
+    nc = tc.nc
+    xb_v = x_bytes.rearrange("b u v k -> (b u) (v k)")
+    w_v = w_span.rearrange("b u v c -> (b u) (v c)")
+    out_v = out.rearrange("b u v o -> (b u) v o")
+
+    with ExitStack() as ctx:
+        const = ctx.enter_context(tc.tile_pool(name="const", bufs=1))
+        prod_pool = ctx.enter_context(tc.tile_pool(name="prodp", bufs=3))
+        xsh_pool = ctx.enter_context(tc.tile_pool(name="xshp", bufs=3))
+        ot_pool = ctx.enter_context(tc.tile_pool(name="otp", bufs=4))
+        osb_pool = ctx.enter_context(tc.tile_pool(name="osbp", bufs=4))
+        ps_a = ctx.enter_context(tc.psum_pool(name="psa", bufs=4))
+        ps_b = ctx.enter_context(tc.psum_pool(name="psb", bufs=1))
+        ps_w = ctx.enter_context(tc.psum_pool(name="psw", bufs=3))
+
+        xb = {}
+        xbf = {}
+        grp = {}
+        prod = {}
+        o_t = {}
+        wps = {}
+        wsb = {}
+        xsh = {}
+
+        w_t = const.tile([P, NV, GRP], BF16, name="w_t", tag="w_t")
+        bias_t = const.tile([P, 2], BF16, name="bias_t", tag="bias_t")
+        ident = const.tile([P, P], F32, name="ident", tag="ident")
+        make_identity(nc, ident[:])
+        ident_bf = const.tile([P, P], BF16, name="ident_bf", tag="ident_bf")
+        make_identity(nc, ident_bf[:])
+        ind = const.tile([P, 2], F32, name="ind", tag="ind")
+        nc.vector.tensor_reduce(out=ind[:, 0:1], in_=ident[:, 0:P:32], axis=mybir.AxisListType.X, op=ADD)
+        nc.vector.tensor_reduce(out=ind[:, 1:2], in_=ident[:, 31:P:32], axis=mybir.AxisListType.X, op=ADD)
+        edge = const.tile([P, 2], F32, name="edge", tag="edge")
+        nc.vector.tensor_scalar(out=edge[:], in0=ind[:], scalar1=-1.0, scalar2=1.0, op0=MULT, op1=ADD)
+        dg = []
+        for e in range(2):
+            t = const.tile([P, P], BF16, name="dg%d" % e, tag="dg%d" % e)
+            nc.vector.tensor_scalar_mul(out=t[:], in0=ident_bf[:], scalar1=edge[:, e : e + 1])
+            dg.append(t)
+        xs1 = const.tile([P, 35 * F], F32, name="xs1", tag="xs1")
+        nc.gpsimd.memset(xs1[:, 0:F], 0.0)
+        nc.gpsimd.memset(xs1[:, 33 * F : 34 * F], 0.0)
+        g_units = sorted(set(job[0] for job in G_JOBS))
+        for k in g_units:
+            wsb[k] = const.tile([P, NB, WCOL], F32, name="wsb%d" % k, tag="wsb%d" % k)
+        xit = []
+        for j in range(3):
+            xit.append(const.tile([P, 2, F], F32, name="xit%d" % j, tag="xit%d" % j))
+        wi_codes = const.tile([P, 2 * F], U32, name="wi_codes", tag="wi_codes", align_bytes=64)
+        wi_sc = const.tile([P, 2 * F], U8, name="wi_sc", tag="wi_sc", align_bytes=64)
+
+        def wcopy(k):
+            n, h = k // 2, k % 2
+            t = ps_w.tile([P, NB, WCOL], F32, name="wps", tag="wps")
+            if h == 0:
+                parts = ((dg[0], 0, 54, 0), (ident_bf, 45, 72, 54))
+            else:
+                parts = ((ident_bf, 72, 99, 0), (dg[1], 90, 144, 27))
+            for lhs, c0, c1, o0 in parts:
+                nc.tensor.matmul(
+                    out=t[:, :, o0 : o0 + c1 - c0],
+                    lhsT=lhs[:],
+                    rhs=w_t[:, NB * n : NB * (n + 1), c0:c1],
+                    start=True,
+                    stop=True,
+                )
+            wps[k] = t
+
+        def wmask(k):
+            n, h = k // 2, k % 2
+            src = w_t[:, NB * n : NB * (n + 1), :]
+            dst = wsb[k]
+            if h == 0:
+                nc.scalar.activation(out=dst[:, :, 0:54], in_=src[:, :, 0:54], func=ACT.Copy, scale=edge[:, 0:1])
+                nc.scalar.copy(out=dst[:, :, 54:81], in_=src[:, :, 45:72])
+            else:
+                nc.scalar.copy(out=dst[:, :, 0:27], in_=src[:, :, 72:99])
+                nc.scalar.activation(out=dst[:, :, 27:81], in_=src[:, :, 90:144], func=ACT.Copy, scale=edge[:, 1:2])
+
+        def rows(who, k):
+            n, h = k // 2, k % 2
+            if who == "g":
+                dst = xsh_pool.tile([P, 7 * F], F32, name="xshg", tag="xshg")
+            else:
+                dst = xsh_pool.tile([P, 7 * F], F32, name="xshv", tag="xshv")
+            xsh[(who, k)] = dst
+            cols = slice(F * NB * n, F * (NB * n + 6))
+            for lo, hi in ((0, 112), (112, 127)):
+                if h == 0:
+                    nc.sync.dma_start(out=dst[lo + 1 : hi + 1, 0 : 6 * F], in_=xs1[lo:hi, cols])
+                else:
+                    nc.sync.dma_start(out=dst[lo:hi, 0 : 6 * F], in_=xs1[lo + 1 : hi + 1, cols])
+            if h == 0:
+                nc.sync.dma_start(out=dst[0:1, 0 : 6 * F], in_=xs1[P - 1 : P, cols])
+            else:
+                nc.sync.dma_start(out=dst[P - 1 : P, 0 : 6 * F], in_=xs1[0:1, cols])
+
+        with ExitStack() as ph1:
+            c1 = ph1.enter_context(tc.tile_pool(name="c1", bufs=1))
+            bytes_pool = ph1.enter_context(tc.tile_pool(name="bytes", bufs=2))
+            xbf_pool = ph1.enter_context(tc.tile_pool(name="xbfp", bufs=3))
+            grp_pool = ph1.enter_context(tc.tile_pool(name="grpp", bufs=3))
+
+            def load(q, parts):
+                t = bytes_pool.tile([P, 4 * C], U8, name="xb", tag="xb")
+                w = 4 * C // parts
+                for s in range(parts):
+                    nc.sync.dma_start(
+                        out=t[:, w * s : w * (s + 1)], in_=xb_v[:, 4 * C * q + w * s : 4 * C * q + w * (s + 1)]
+                    )
+                xb[q] = t
+
+            scale_bc = c1.tile([P, C], F32, name="scale_bc", tag="scale_bc")
+            nc.scalar.dma_start(
+                out=scale_bc[:], in_=x_scale.rearrange("a b c k -> (a b c k)").partition_broadcast(P)
+            )
+            load(0, 4)
+            wi_raw = prod_pool.tile([P, 2, 4, F], BF16, name="wi_raw", tag="pd", align_bytes=64)
+            nc.sync.dma_start(out=wi_raw[:], in_=Wi.rearrange("(g p t) n -> p g t n", p=P, t=4))
+            with nc.allow_non_contiguous_dma(reason="256 bias values, one to a partition"):
+                nc.sync.dma_start(out=bias_t[:], in_=bi.rearrange("(h p) -> p h", p=P))
+            load(1, 1)
+            nc.sync.dma_start(out=w_t[:].rearrange("p v c -> p (v c)"), in_=w_v)
+
+            wi_grp = prod_pool.tile([P, 2, F, 4], BF16, name="wi_grp", tag="pd", align_bytes=64)
+            nc.scalar.copy(out=wi_grp[:], in_=wi_raw[:].rearrange("p g t n -> p g n t"))
+            nc.vector.quantize_mx(
+                out=wi_codes[:].bitcast(FP8X4), scales=wi_sc[:], in_=wi_grp[:].rearrange("p g n t -> p (g n t)")
+            )
+
+            def fp8_of(v):
+                return xb[v // 4][:, C * (v % 4) : C * (v % 4 + 1)].bitcast(FP8)
+
+            def widen(c):
+                for v in (2 * c, 2 * c + 1):
+                    t = xbf_pool.tile([P, C], BF16, name="xbf", tag="xbf")
+                    nc.vector.tensor_tensor(out=t[:], in0=fp8_of(v), in1=scale_bc[:], op=MULT)
+                    xbf[v] = t
+
+            def xpose(c):
+                g_t = grp_pool.tile([P, 2048], BF16, name="grp", tag="grp", align_bytes=64)
+                grp[c] = g_t
+                gw = g_t[:].bitcast(F32).rearrange("p (g r u) -> p g r u", g=2, u=2)
+                for vl in range(2):
+                    words = xbf[2 * c + vl][:].bitcast(F32)
+                    xt = ps_a.tile([P, 2, 2, P], F32, name="xt", tag="a")
+                    for g in range(2):
+                        for u in range(2):
+                            nc.tensor.transpose(xt[:, g, u, :], words[:, 256 * g + u : 256 * (g + 1) : 2], ident[:])
+                    nc.scalar.copy(out=gw[:, :, P * vl : P * (vl + 1), :], in_=xt[:].rearrange("p g u r -> p g r u"))
+
+            def quant_mm(c):
+                codes = grp_pool.tile([P, 512], U32, name="codes", tag="codes", align_bytes=64)
+                sc = grp_pool.tile([P, 512], U8, name="sc", tag="sc", align_bytes=64)
+                nc.vector.quantize_mx(out=codes[:].bitcast(FP8X4), scales=sc[:], in_=grp[c][:])
+                mmp = ps_b.tile([P, 2, F], F32, name="mmp", tag="b")
+                for h in range(2):
+                    for g in range(2):
+                        wcols = slice(F * g + P * h, F * g + P * (h + 1))
+                        xcols = slice(F * g, F * (g + 1))
+                        nc.tensor.matmul_mx(
+                            out=mmp[:, h, :],
+                            lhsT=wi_codes[:, wcols].bitcast(FP8X4),
+                            lhsT_scale=wi_sc[:, wcols],
+                            rhs=codes[:, xcols].bitcast(FP8X4),
+                            rhs_scale=sc[:, xcols],
+                            start=(g == 0),
+                            stop=(g == 1),
+                        )
+                for h in range(2):
+                    nc.scalar.activation(
+                        out=xit[c % 3][:, h, :],
+                        in_=mmp[:, h, :],
+                        func=ACT.Identity,
+                        bias=bias_t[:, h : h + 1],
+                        scale=1.0,
+                    )
+
+            def turn(c):
+                pt = ps_a.tile([P, 2, F], F32, name="pt", tag="a")
+                for vl in range(2):
+                    for h in range(2):
+                        nc.tensor.transpose(
+                            pt[:, vl, P * h : P * (h + 1)], xit[c % 3][:, h, P * vl : P * (vl + 1)], ident[:]
+                        )
+                nc.scalar.copy(out=xs1[:, F * (1 + 2 * c) : F * (3 + 2 * c)], in_=pt[:].rearrange("p a c -> p (a c)"))
+
+            early = [("g", k) for k in g_units[0:3]] + [("v", job[0]) for job in V_JOBS[0:3]]
+            for t in range(NCH + 3):
+                if t < NCH:
+                    widen(t)
+                    xpose(t)
+                if t % 2 == 1 and t // 2 + 2 < NV // 4:
+                    load(t // 2 + 2, 1)
+                if 0 <= t - 2 < NCH:
+                    quant_mm(t - 2)
+                if 0 <= t - 3 < NCH:
+                    c = t - 3
+                    turn(c)
+                    for who, k in early:
+                        if c == min(k // 2 * 2 + 2, NCH - 1):
+                            rows(who, k)
+                if 3 <= t < 3 + len(g_units):
+                    wmask(g_units[t - 3])
+                if t == 3 + len(g_units):
+                    for job in V_JOBS[0:3]:
+                        wcopy(job[0])
+
+        with ExitStack() as ph2:
+            gm_pool = ph2.enter_context(tc.tile_pool(name="gmp", bufs=3, reuse_waits="tile"))
+
+            def source(who, job, lo, ln):
+                k, a0, na = job
+                i = lo // ROW3
+                if i == 1:
+                    src, st = xs1, F * NB * (k // 2) + lo - ROW3
+                else:
+                    src, st = xsh[(who, k)], lo - ROW3 * i
+                return src[:, st : st + F * NB].rearrange("p (a c) -> p a c", c=F)[:, a0 : a0 + na, 0:ln]
+
+            def block(h, lo):
+                i, g = lo // ROW3, lo // GRP
+                if h == 0:
+                    return g if i == 0 else g + 1
+                return g - 8 if i == 1 else g - 7
+
+            def mult(who, job):
+                k, a0, na = job
+                h = k % 2
+                if who == "v":
+                    eng = nc.vector
+                    pd = prod_pool.tile([P, NB, HALF], F32, name="pd", tag="pd", align_bytes=64)
+                    wk = wps[k][:, a0 : a0 + na]
+                else:
+                    eng = nc.gpsimd
+                    pd = gm_pool.tile([P, NB, HALF], F32, name="gm", tag="gm")
+                    wk = wsb[k][:, a0 : a0 + na]
+                prod[job] = pd
+                for lo, hi, whole in pieces(h):
+                    ln = hi - lo
+                    win = source(who, job, lo, ln)
+                    dst = pd[:, 0:na, lo - HALF * h : hi - HALF * h]
+                    w0 = TAPS * block(h, lo)
+                    if whole:
+                        nj = ln // TAPS
+                        eng.tensor_tensor(
+                            out=dst.rearrange("p a (j m) -> p a j m", m=TAPS),
+                            in0=win.rearrange("p a (j m) -> p a j m", m=TAPS),
+                            in1=wk[:, :, w0 : w0 + TAPS].unsqueeze(2).to_broadcast([P, na, nj, TAPS]),
+                            op=MULT,
+                        )
+                    else:
+                        m0 = lo % TAPS
+                        eng.tensor_tensor(out=dst, in0=win, in1=wk[:, :, w0 + m0 : w0 + m0 + ln], op=MULT)
+
+            def store(queue, job, t):
+                k, a0, na = job
+                n, h = k // 2, k % 2
+                queue.dma_start(
+                    out=out_v[:, NB * n + a0 : NB * n + a0 + na, P * h : P * (h + 1)], in_=t[:, 0:na, :]
+                )
+
+            def tapsum_pe(job):
+                na = job[2]
+                pd = prod[job]
+                acc = ps_a.tile([P, NB, P], F32, name="acc", tag="a")
+                for a in range(na):
+                    for m in range(TAPS):
+                        nc.tensor.matmul(
+                            out=acc[:, a, :],
+                            lhsT=pd[:, a, m : m + TAPS * (P - 1) + 1 : TAPS],
+                            rhs=ident[:],
+                            is_transpose=True,
+                            start=(m == 0),
+                            stop=(m == TAPS - 1),
+                        )
+                t = ot_pool.tile([P, NB, P], F32, name="o_t", tag="o_t")
+                nc.scalar.copy(out=t[:, 0:na, :], in_=acc[:, 0:na, :])
+                o_t[job] = t
+
+            def back(job):
+                na = job[2]
+                ob = ps_b.tile([P, NB, P], F32, name="ob", tag="b")
+                for a in range(na):
+                    nc.tensor.transpose(ob[:, a, :], o_t[job][:, a, :], ident[:])
+                t = osb_pool.tile([P, NB, P], F32, name="osb", tag="osb")
+                nc.scalar.copy(out=t[:, 0:na, :], in_=ob[:, 0:na, :])
+                store(nc.scalar, job, t)
+
+            def tapsum_v(job):
+                k, a0, na = job
+                pv = prod[job][:].rearrange("p a (o m) -> p a o m", m=TAPS)
+                for a in range(0, na, 2):
+                    t = osb_pool.tile([P, 2, P], F32, name="osv", tag="osv")
+                    nc.vector.tensor_reduce(out=t[:, 0:2, :], in_=pv[:, a : a + 2], axis=mybir.AxisListType.X, op=ADD)
+                    store(nc.sync, (k, a0 + a, 2), t)
+
+            ticks = []
+            for i in range(len(V_JOBS)):
+                ticks.append(("mult", i))
+                if V_JOBS[i] in V_SUM:
+                    ticks.append(("sum", i))
+            for job in G_JOBS[0:3]:
+                mult("g", job)
+            pend = []
+            for tick in range(len(ticks) + 2):
+                todo = []
+                if tick < len(ticks):
+                    what, i = ticks[tick]
+                    job = V_JOBS[i]
+                    if what == "sum":
+                        tapsum_v(job)
+                    else:
+                        mult("v", job)
+                        if i + 3 < len(V_JOBS) and ("v", V_JOBS[i + 3][0]) not in xsh:
+                            rows("v", V_JOBS[i + 3][0])
+                            wcopy(V_JOBS[i + 3][0])
+                        if job not in V_SUM:
+                            todo.append(job)
+                for job in pend:
+                    back(job)
+                for i in range(len(G_JOBS)):
+                    if G_AFTER[i] == tick:
+                        todo.append(G_JOBS[i])
+                for job in todo:
+                    tapsum_pe(job)
+                    if job in G_JOBS and G_JOBS.index(job) + 3 < len(G_JOBS):
+                        nxt = G_JOBS[G_JOBS.index(job) + 3]
+                        if ("g", nxt[0]) not in xsh:
+                            rows("g", nxt[0])
+                        mult("g", nxt)
+                pend = todo
+            for job in pend:
+                back(job)

@@ -26,13 +26,12 @@ HALF = 1152
 NB = 4
 NCH = NV // 2
 WCOL = 81
-G_JOBS = ((0, 0, 4), (1, 0, 4), (2, 0, 4), (3, 0, 4), (4, 0, 4), (5, 0, 2))
-G_AFTER = (3, 5, 8, 10, 14, 16)
+G_JOBS = ((0, 0, 4), (1, 0, 4), (2, 0, 4), (3, 0, 4), (4, 0, 4), (5, 0, 4))
+G_AFTER = (3, 5, 8, 10, 13, 15)
 V_JOBS = (
-    (5, 2, 2), (6, 0, 4), (7, 0, 4), (8, 0, 4), (9, 0, 4), (10, 0, 4), (11, 0, 4), (12, 0, 4),
-    (13, 0, 2), (13, 2, 2), (14, 0, 4), (15, 0, 4),
+    (6, 0, 4), (7, 0, 4), (8, 0, 4), (9, 0, 4), (10, 0, 4), (11, 0, 4), (12, 0, 4), (13, 0, 4), (14, 0, 4), (15, 0, 4),
 )
-V_SUM = ((7, 0, 4), (9, 0, 4), (11, 0, 4), (13, 2, 2), (14, 0, 4), (15, 0, 4))
+V_SUM = ((7, 0, 4), (8, 0, 4), (10, 0, 4), (11, 0, 4), (13, 0, 4), (14, 0, 4), (15, 0, 4))
 
 
 def pieces(h):

@@ -22,22 +22,24 @@ F = 256
 TAPS = 9
 GRP = 144
 ROW3 = 768
-HALF = 1152
-NB = 4
+QO = 64
+QF = QO * TAPS
+NB = 8
 NCH = NV // 2
-WCOL = 81
-G_JOBS = ((0, 0, 4), (1, 0, 4), (2, 0, 4), (3, 0, 4), (4, 0, 4), (5, 0, 4))
-G_AFTER = (3, 5, 8, 10, 13, 15)
+WCOL = 45
+G_JOBS = ((0, 0, 8), (1, 0, 8), (2, 0, 8), (3, 0, 8), (4, 0, 8), (5, 0, 8))
+G_AFTER = (3, 5, 7, 9, 11, 13)
 V_JOBS = (
-    (6, 0, 4), (7, 0, 4), (8, 0, 4), (9, 0, 4), (10, 0, 4), (11, 0, 4), (12, 0, 4), (13, 0, 4), (14, 0, 4), (15, 0, 4),
+    (6, 0, 8), (7, 0, 8), (8, 0, 8), (9, 0, 8), (10, 0, 8), (11, 0, 8), (12, 0, 8),
+    (13, 0, 4), (13, 4, 4), (14, 0, 8), (15, 0, 8),
 )
-V_SUM = ((7, 0, 4), (8, 0, 4), (10, 0, 4), (11, 0, 4), (13, 0, 4), (14, 0, 4), (15, 0, 4))
+V_SUM = ((7, 0, 8), (8, 0, 8), (10, 0, 8), (11, 0, 8), (13, 4, 4), (14, 0, 8), (15, 0, 8))
 
 
-def pieces(h):
+def pieces(q):
     res = []
-    f = HALF * h
-    end = HALF * (h + 1)
+    f = QF * q
+    end = QF * (q + 1)
     while f < end:
         nxt = min(end, (f // GRP + 1) * GRP, (f // ROW3 + 1) * ROW3)
         lo = f
@@ -54,6 +56,25 @@ def pieces(h):
     return res
 
 
+def blocks(q):
+    res = []
+    for lo, hi, whole in pieces(q):
+        pair = (lo // GRP, lo // ROW3)
+        if pair not in res:
+            res.append(pair)
+    return res
+
+
+def runs(q):
+    res = []
+    for b, (g, i) in enumerate(blocks(q)):
+        if res and res[-1][0] == i:
+            res[-1] = (i, res[-1][1], res[-1][2] + 1, res[-1][3])
+        else:
+            res.append((i, b, 1, g))
+    return res
+
+
 def tile_involution2d_pa_kernel(tc, x_bytes, x_scale, Wi, bi, w_span, out):
     nc = tc.nc
     xb_v = x_bytes.rearrange("b u v k -> (b u) (v k)")
@@ -63,7 +84,7 @@ def tile_involution2d_pa_kernel(tc, x_bytes, x_scale, Wi, bi, w_span, out):
     with ExitStack() as ctx:
         const = ctx.enter_context(tc.tile_pool(name="const", bufs=1))
         prod_pool = ctx.enter_context(tc.tile_pool(name="prodp", bufs=3))
-        xsh_pool = ctx.enter_context(tc.tile_pool(name="xshp", bufs=3))
+        xsh_pool = ctx.enter_context(tc.tile_pool(name="xshp", bufs=2))
         ot_pool = ctx.enter_context(tc.tile_pool(name="otp", bufs=4))
         osb_pool = ctx.enter_context(tc.tile_pool(name="osbp", bufs=4))
         ps_a = ctx.enter_context(tc.psum_pool(name="psa", bufs=4))
@@ -95,6 +116,7 @@ def tile_involution2d_pa_kernel(tc, x_bytes, x_scale, Wi, bi, w_span, out):
             t = const.tile([P, P], BF16, name="dg%d" % e, tag="dg%d" % e)
             nc.vector.tensor_scalar_mul(out=t[:], in0=ident_bf[:], scalar1=edge[:, e : e + 1])
             dg.append(t)
+        wdiag = (dg[0], ident_bf, dg[1])
         xs1 = const.tile([P, 35 * F], F32, name="xs1", tag="xs1")
         nc.gpsimd.memset(xs1[:, 0:F], 0.0)
         nc.gpsimd.memset(xs1[:, 33 * F : 34 * F], 0.0)
@@ -108,50 +130,47 @@ def tile_involution2d_pa_kernel(tc, x_bytes, x_scale, Wi, bi, w_span, out):
         wi_sc = const.tile([P, 2 * F], U8, name="wi_sc", tag="wi_sc", align_bytes=64)
 
         def wcopy(k):
-            n, h = k // 2, k % 2
+            n, q = k // 4, k % 4
             t = ps_w.tile([P, NB, WCOL], F32, name="wps", tag="wps")
-            if h == 0:
-                parts = ((dg[0], 0, 54, 0), (ident_bf, 45, 72, 54))
-            else:
-                parts = ((ident_bf, 72, 99, 0), (dg[1], 90, 144, 27))
-            for lhs, c0, c1, o0 in parts:
+            for i, b0, nb, g0 in runs(q):
                 nc.tensor.matmul(
-                    out=t[:, :, o0 : o0 + c1 - c0],
-                    lhsT=lhs[:],
-                    rhs=w_t[:, NB * n : NB * (n + 1), c0:c1],
+                    out=t[:, :, TAPS * b0 : TAPS * (b0 + nb)],
+                    lhsT=wdiag[i][:],
+                    rhs=w_t[:, NB * n : NB * (n + 1), TAPS * g0 : TAPS * (g0 + nb)],
                     start=True,
                     stop=True,
                 )
             wps[k] = t
 
         def wmask(k):
-            n, h = k // 2, k % 2
-            src = w_t[:, NB * n : NB * (n + 1), :]
-            dst = wsb[k]
-            if h == 0:
-                nc.scalar.activation(out=dst[:, :, 0:54], in_=src[:, :, 0:54], func=ACT.Copy, scale=edge[:, 0:1])
-                nc.scalar.copy(out=dst[:, :, 54:81], in_=src[:, :, 45:72])
-            else:
-                nc.scalar.copy(out=dst[:, :, 0:27], in_=src[:, :, 72:99])
-                nc.scalar.activation(out=dst[:, :, 27:81], in_=src[:, :, 90:144], func=ACT.Copy, scale=edge[:, 1:2])
+            n, q = k // 4, k % 4
+            for i, b0, nb, g0 in runs(q):
+                src = w_t[:, NB * n : NB * (n + 1), TAPS * g0 : TAPS * (g0 + nb)]
+                dst = wsb[k][:, :, TAPS * b0 : TAPS * (b0 + nb)]
+                if i == 1:
+                    nc.scalar.copy(out=dst, in_=src)
+                else:
+                    nc.scalar.activation(out=dst, in_=src, func=ACT.Copy, scale=edge[:, i // 2 : i // 2 + 1])
 
         def rows(who, k):
-            n, h = k // 2, k % 2
+            n, d = k // 4, k % 4 // 2
+            if (who, n, d) in xsh:
+                return
             if who == "g":
-                dst = xsh_pool.tile([P, 7 * F], F32, name="xshg", tag="xshg")
+                dst = xsh_pool.tile([P, 11 * F], F32, name="xshg", tag="xshg")
             else:
-                dst = xsh_pool.tile([P, 7 * F], F32, name="xshv", tag="xshv")
-            xsh[(who, k)] = dst
-            cols = slice(F * NB * n, F * (NB * n + 6))
+                dst = xsh_pool.tile([P, 11 * F], F32, name="xshv", tag="xshv")
+            xsh[(who, n, d)] = dst
+            cols = slice(F * NB * n, F * (NB * n + 10))
             for lo, hi in ((0, 112), (112, 127)):
-                if h == 0:
-                    nc.sync.dma_start(out=dst[lo + 1 : hi + 1, 0 : 6 * F], in_=xs1[lo:hi, cols])
+                if d == 0:
+                    nc.sync.dma_start(out=dst[lo + 1 : hi + 1, 0 : 10 * F], in_=xs1[lo:hi, cols])
                 else:
-                    nc.sync.dma_start(out=dst[lo:hi, 0 : 6 * F], in_=xs1[lo + 1 : hi + 1, cols])
-            if h == 0:
-                nc.sync.dma_start(out=dst[0:1, 0 : 6 * F], in_=xs1[P - 1 : P, cols])
+                    nc.sync.dma_start(out=dst[lo:hi, 0 : 10 * F], in_=xs1[lo + 1 : hi + 1, cols])
+            if d == 0:
+                nc.sync.dma_start(out=dst[0:1, 0 : 10 * F], in_=xs1[P - 1 : P, cols])
             else:
-                nc.sync.dma_start(out=dst[P - 1 : P, 0 : 6 * F], in_=xs1[0:1, cols])
+                nc.sync.dma_start(out=dst[P - 1 : P, 0 : 10 * F], in_=xs1[0:1, cols])
 
         with ExitStack() as ph1:
             c1 = ph1.enter_context(tc.tile_pool(name="c1", bufs=1))
@@ -168,9 +187,9 @@ def tile_involution2d_pa_kernel(tc, x_bytes, x_scale, Wi, bi, w_span, out):
                     )
                 xb[q] = t
 
-            scale_bc = c1.tile([P, C], F32, name="scale_bc", tag="scale_bc")
+            scale_bc = c1.tile([P, 2 * C], F32, name="scale_bc", tag="scale_bc")
             nc.scalar.dma_start(
-                out=scale_bc[:], in_=x_scale.rearrange("a b c k -> (a b c k)").partition_broadcast(P)
+                out=scale_bc[:, 0:C], in_=x_scale.rearrange("a b c k -> (a b c k)").partition_broadcast(P)
             )
             load(0, 4)
             wi_raw = prod_pool.tile([P, 2, 4, F], BF16, name="wi_raw", tag="pd", align_bytes=64)
@@ -180,27 +199,30 @@ def tile_involution2d_pa_kernel(tc, x_bytes, x_scale, Wi, bi, w_span, out):
             load(1, 1)
             nc.sync.dma_start(out=w_t[:].rearrange("p v c -> p (v c)"), in_=w_v)
 
+            nc.scalar.copy(out=scale_bc[:, C : 2 * C], in_=scale_bc[:, 0:C])
             wi_grp = prod_pool.tile([P, 2, F, 4], BF16, name="wi_grp", tag="pd", align_bytes=64)
             nc.scalar.copy(out=wi_grp[:], in_=wi_raw[:].rearrange("p g t n -> p g n t"))
             nc.vector.quantize_mx(
                 out=wi_codes[:].bitcast(FP8X4), scales=wi_sc[:], in_=wi_grp[:].rearrange("p g n t -> p (g n t)")
             )
 
-            def fp8_of(v):
-                return xb[v // 4][:, C * (v % 4) : C * (v % 4 + 1)].bitcast(FP8)
-
             def widen(c):
-                for v in (2 * c, 2 * c + 1):
-                    t = xbf_pool.tile([P, C], BF16, name="xbf", tag="xbf")
-                    nc.vector.tensor_tensor(out=t[:], in0=fp8_of(v), in1=scale_bc[:], op=MULT)
-                    xbf[v] = t
+                t = xbf_pool.tile([P, 2 * C], BF16, name="xbf", tag="xbf")
+                xbf[c] = t
+                src = xb[c // 2][:, 2 * C * (c % 2) : 2 * C * (c % 2 + 1)].bitcast(FP8)
+                if c == 0:
+                    for vl in range(2):
+                        cols = slice(C * vl, C * (vl + 1))
+                        nc.vector.tensor_tensor(out=t[:, cols], in0=src[:, cols], in1=scale_bc[:, 0:C], op=MULT)
+                else:
+                    nc.vector.tensor_tensor(out=t[:], in0=src, in1=scale_bc[:], op=MULT)
 
             def xpose(c):
                 g_t = grp_pool.tile([P, 2048], BF16, name="grp", tag="grp", align_bytes=64)
                 grp[c] = g_t
                 gw = g_t[:].bitcast(F32).rearrange("p (g r u) -> p g r u", g=2, u=2)
                 for vl in range(2):
-                    words = xbf[2 * c + vl][:].bitcast(F32)
+                    words = xbf[c][:, C * vl : C * (vl + 1)].bitcast(F32)
                     xt = ps_a.tile([P, 2, 2, P], F32, name="xt", tag="a")
                     for g in range(2):
                         for u in range(2):
@@ -243,7 +265,7 @@ def tile_involution2d_pa_kernel(tc, x_bytes, x_scale, Wi, bi, w_span, out):
                         )
                 nc.scalar.copy(out=xs1[:, F * (1 + 2 * c) : F * (3 + 2 * c)], in_=pt[:].rearrange("p a c -> p (a c)"))
 
-            early = [("g", k) for k in g_units[0:3]] + [("v", job[0]) for job in V_JOBS[0:3]]
+            early = [("g", k) for k in g_units[0:4]] + [("v", job[0]) for job in V_JOBS[0:3]]
             for t in range(NCH + 3):
                 if t < NCH:
                     widen(t)
@@ -256,7 +278,7 @@ def tile_involution2d_pa_kernel(tc, x_bytes, x_scale, Wi, bi, w_span, out):
                     c = t - 3
                     turn(c)
                     for who, k in early:
-                        if c == min(k // 2 * 2 + 2, NCH - 1):
+                        if c == min(k // 4 * 4 + 4, NCH - 1):
                             rows(who, k)
                 if 3 <= t < 3 + len(g_units):
                     wmask(g_units[t - 3])
@@ -271,34 +293,28 @@ def tile_involution2d_pa_kernel(tc, x_bytes, x_scale, Wi, bi, w_span, out):
                 k, a0, na = job
                 i = lo // ROW3
                 if i == 1:
-                    src, st = xs1, F * NB * (k // 2) + lo - ROW3
+                    src, st = xs1, F * NB * (k // 4) + lo - ROW3
                 else:
-                    src, st = xsh[(who, k)], lo - ROW3 * i
+                    src, st = xsh[(who, k // 4, i // 2)], lo - ROW3 * i
                 return src[:, st : st + F * NB].rearrange("p (a c) -> p a c", c=F)[:, a0 : a0 + na, 0:ln]
-
-            def block(h, lo):
-                i, g = lo // ROW3, lo // GRP
-                if h == 0:
-                    return g if i == 0 else g + 1
-                return g - 8 if i == 1 else g - 7
 
             def mult(who, job):
                 k, a0, na = job
-                h = k % 2
+                q = k % 4
                 if who == "v":
                     eng = nc.vector
-                    pd = prod_pool.tile([P, NB, HALF], F32, name="pd", tag="pd", align_bytes=64)
+                    pd = prod_pool.tile([P, NB, QF], F32, name="pd", tag="pd", align_bytes=64)
                     wk = wps[k][:, a0 : a0 + na]
                 else:
                     eng = nc.gpsimd
-                    pd = gm_pool.tile([P, NB, HALF], F32, name="gm", tag="gm")
+                    pd = gm_pool.tile([P, NB, QF], F32, name="gm", tag="gm")
                     wk = wsb[k][:, a0 : a0 + na]
                 prod[job] = pd
-                for lo, hi, whole in pieces(h):
+                for lo, hi, whole in pieces(q):
                     ln = hi - lo
                     win = source(who, job, lo, ln)
-                    dst = pd[:, 0:na, lo - HALF * h : hi - HALF * h]
-                    w0 = TAPS * block(h, lo)
+                    dst = pd[:, 0:na, lo - QF * q : hi - QF * q]
+                    w0 = TAPS * blocks(q).index((lo // GRP, lo // ROW3))
                     if whole:
                         nj = ln // TAPS
                         eng.tensor_tensor(
@@ -313,45 +329,51 @@ def tile_involution2d_pa_kernel(tc, x_bytes, x_scale, Wi, bi, w_span, out):
 
             def store(queue, job, t):
                 k, a0, na = job
-                n, h = k // 2, k % 2
+                n, q = k // 4, k % 4
                 queue.dma_start(
-                    out=out_v[:, NB * n + a0 : NB * n + a0 + na, P * h : P * (h + 1)], in_=t[:, 0:na, :]
+                    out=out_v[:, NB * n + a0 : NB * n + a0 + na, QO * q : QO * (q + 1)], in_=t[:, 0:na, :]
                 )
 
             def tapsum_pe(job):
-                na = job[2]
-                pd = prod[job]
-                acc = ps_a.tile([P, NB, P], F32, name="acc", tag="a")
-                for a in range(na):
+                npair = job[2] // 2
+                flat = prod[job][:].rearrange("p a f -> p (a f)")
+                acc = ps_a.tile([P, NB // 2, P], F32, name="acc", tag="a")
+                for r in range(npair):
                     for m in range(TAPS):
+                        f0 = 2 * QF * r + m
                         nc.tensor.matmul(
-                            out=acc[:, a, :],
-                            lhsT=pd[:, a, m : m + TAPS * (P - 1) + 1 : TAPS],
+                            out=acc[:, r, :],
+                            lhsT=flat[:, f0 : f0 + TAPS * (P - 1) + 1 : TAPS],
                             rhs=ident[:],
                             is_transpose=True,
                             start=(m == 0),
                             stop=(m == TAPS - 1),
                         )
-                t = ot_pool.tile([P, NB, P], F32, name="o_t", tag="o_t")
-                nc.scalar.copy(out=t[:, 0:na, :], in_=acc[:, 0:na, :])
+                t = ot_pool.tile([P, NB // 2, P], F32, name="o_t", tag="o_t")
+                nc.scalar.copy(out=t[:, 0:npair, :], in_=acc[:, 0:npair, :])
                 o_t[job] = t
 
             def back(job):
                 na = job[2]
-                ob = ps_b.tile([P, NB, P], F32, name="ob", tag="b")
-                for a in range(na):
-                    nc.tensor.transpose(ob[:, a, :], o_t[job][:, a, :], ident[:])
-                t = osb_pool.tile([P, NB, P], F32, name="osb", tag="osb")
-                nc.scalar.copy(out=t[:, 0:na, :], in_=ob[:, 0:na, :])
+                npair = na // 2
+                ob = ps_b.tile([P, NB // 2, P], F32, name="ob", tag="b")
+                for r in range(npair):
+                    nc.tensor.transpose(ob[:, r, :], o_t[job][:, r, :], ident[:])
+                t = osb_pool.tile([P, NB, QO], F32, name="osb", tag="osb")
+                nc.scalar.copy(
+                    out=t[:, 0:na, :].rearrange("p a o -> p (a o)"), in_=ob[:, 0:npair, :].rearrange("p r c -> p (r c)")
+                )
                 store(nc.scalar, job, t)
 
-            def tapsum_v(job):
+            def tapsum_v(job, step):
                 k, a0, na = job
                 pv = prod[job][:].rearrange("p a (o m) -> p a o m", m=TAPS)
-                for a in range(0, na, 2):
-                    t = osb_pool.tile([P, 2, P], F32, name="osv", tag="osv")
-                    nc.vector.tensor_reduce(out=t[:, 0:2, :], in_=pv[:, a : a + 2], axis=mybir.AxisListType.X, op=ADD)
-                    store(nc.sync, (k, a0 + a, 2), t)
+                for a in range(0, na, step):
+                    t = osb_pool.tile([P, NB, QO], F32, name="osv", tag="osv")
+                    nc.vector.tensor_reduce(
+                        out=t[:, 0:step, :], in_=pv[:, a : a + step], axis=mybir.AxisListType.X, op=ADD
+                    )
+                    store(nc.sync, (k, a0 + a, step), t)
 
             ticks = []
             for i in range(len(V_JOBS)):
@@ -367,10 +389,13 @@ def tile_involution2d_pa_kernel(tc, x_bytes, x_scale, Wi, bi, w_span, out):
                     what, i = ticks[tick]
                     job = V_JOBS[i]
                     if what == "sum":
-                        tapsum_v(job)
+                        if i == len(V_JOBS) - 1:
+                            tapsum_v(job, 2)
+                        else:
+                            tapsum_v(job, job[2])
                     else:
                         mult("v", job)
-                        if i + 3 < len(V_JOBS) and ("v", V_JOBS[i + 3][0]) not in xsh:
+                        if i + 3 < len(V_JOBS) and V_JOBS[i + 3][0] not in wps:
                             rows("v", V_JOBS[i + 3][0])
                             wcopy(V_JOBS[i + 3][0])
                         if job not in V_SUM:
@@ -384,8 +409,7 @@ def tile_involution2d_pa_kernel(tc, x_bytes, x_scale, Wi, bi, w_span, out):
                     tapsum_pe(job)
                     if job in G_JOBS and G_JOBS.index(job) + 3 < len(G_JOBS):
                         nxt = G_JOBS[G_JOBS.index(job) + 3]
-                        if ("g", nxt[0]) not in xsh:
-                            rows("g", nxt[0])
+                        rows("g", nxt[0])
                         mult("g", nxt)
                 pend = todo
             for job in pend:

@@ -27,13 +27,10 @@ QF = QO * TAPS
 NB = 8
 NCH = NV // 2
 WCOL = 45
-G_JOBS = ((0, 0, 8), (1, 0, 8), (2, 0, 8), (3, 0, 8), (4, 0, 8), (5, 0, 8))
-G_AFTER = (3, 5, 7, 9, 11, 13)
-V_JOBS = (
-    (6, 0, 8), (7, 0, 8), (8, 0, 8), (9, 0, 8), (10, 0, 8), (11, 0, 8), (12, 0, 8),
-    (13, 0, 4), (13, 4, 4), (14, 0, 8), (15, 0, 8),
-)
-V_SUM = ((7, 0, 8), (8, 0, 8), (10, 0, 8), (11, 0, 8), (13, 4, 4), (14, 0, 8), (15, 0, 8))
+G_UNITS = (0, 1, 2, 3, 4, 5)
+V_UNITS = (6, 7, 8, 9, 10, 11, 12, 13, 14, 15)
+V_SUM = (8, 10, 12, 13, 14, 15)
+PE_ORDER = (6, 7, 0, 9, 1, 11, 2, 3, 4, 5)
 
 
 def pieces(q):
@@ -120,7 +117,7 @@ def tile_involution2d_pa_kernel(tc, x_bytes, x_scale, Wi, bi, w_span, out):
         xs1 = const.tile([P, 35 * F], F32, name="xs1", tag="xs1")
         nc.gpsimd.memset(xs1[:, 0:F], 0.0)
         nc.gpsimd.memset(xs1[:, 33 * F : 34 * F], 0.0)
-        g_units = sorted(set(job[0] for job in G_JOBS))
+        g_units = G_UNITS
         for k in g_units:
             wsb[k] = const.tile([P, NB, WCOL], F32, name="wsb%d" % k, tag="wsb%d" % k)
         xit = []
@@ -265,7 +262,7 @@ def tile_involution2d_pa_kernel(tc, x_bytes, x_scale, Wi, bi, w_span, out):
                         )
                 nc.scalar.copy(out=xs1[:, F * (1 + 2 * c) : F * (3 + 2 * c)], in_=pt[:].rearrange("p a c -> p (a c)"))
 
-            early = [("g", k) for k in g_units[0:4]] + [("v", job[0]) for job in V_JOBS[0:3]]
+            early = [("g", k) for k in g_units[0:4]] + [("v", k) for k in V_UNITS[0:3]]
             for t in range(NCH + 3):
                 if t < NCH:
                     widen(t)
@@ -283,62 +280,58 @@ def tile_involution2d_pa_kernel(tc, x_bytes, x_scale, Wi, bi, w_span, out):
                 if 3 <= t < 3 + len(g_units):
                     wmask(g_units[t - 3])
                 if t == 3 + len(g_units):
-                    for job in V_JOBS[0:3]:
-                        wcopy(job[0])
+                    for k in V_UNITS[0:2]:
+                        wcopy(k)
 
         with ExitStack() as ph2:
             gm_pool = ph2.enter_context(tc.tile_pool(name="gmp", bufs=3, reuse_waits="tile"))
 
-            def source(who, job, lo, ln):
-                k, a0, na = job
+            def source(who, k, lo, ln):
                 i = lo // ROW3
                 if i == 1:
                     src, st = xs1, F * NB * (k // 4) + lo - ROW3
                 else:
                     src, st = xsh[(who, k // 4, i // 2)], lo - ROW3 * i
-                return src[:, st : st + F * NB].rearrange("p (a c) -> p a c", c=F)[:, a0 : a0 + na, 0:ln]
+                return src[:, st : st + F * NB].rearrange("p (a c) -> p a c", c=F)[:, :, 0:ln]
 
-            def mult(who, job):
-                k, a0, na = job
+            def mult(who, k):
                 q = k % 4
                 if who == "v":
                     eng = nc.vector
                     pd = prod_pool.tile([P, NB, QF], F32, name="pd", tag="pd", align_bytes=64)
-                    wk = wps[k][:, a0 : a0 + na]
+                    wk = wps[k]
                 else:
                     eng = nc.gpsimd
                     pd = gm_pool.tile([P, NB, QF], F32, name="gm", tag="gm")
-                    wk = wsb[k][:, a0 : a0 + na]
-                prod[job] = pd
+                    wk = wsb[k]
+                prod[k] = pd
                 for lo, hi, whole in pieces(q):
                     ln = hi - lo
-                    win = source(who, job, lo, ln)
-                    dst = pd[:, 0:na, lo - QF * q : hi - QF * q]
+                    win = source(who, k, lo, ln)
+                    dst = pd[:, :, lo - QF * q : hi - QF * q]
                     w0 = TAPS * blocks(q).index((lo // GRP, lo // ROW3))
                     if whole:
                         nj = ln // TAPS
                         eng.tensor_tensor(
                             out=dst.rearrange("p a (j m) -> p a j m", m=TAPS),
                             in0=win.rearrange("p a (j m) -> p a j m", m=TAPS),
-                            in1=wk[:, :, w0 : w0 + TAPS].unsqueeze(2).to_broadcast([P, na, nj, TAPS]),
+                            in1=wk[:, :, w0 : w0 + TAPS].unsqueeze(2).to_broadcast([P, NB, nj, TAPS]),
                             op=MULT,
                         )
                     else:
                         m0 = lo % TAPS
                         eng.tensor_tensor(out=dst, in0=win, in1=wk[:, :, w0 + m0 : w0 + m0 + ln], op=MULT)
 
-            def store(queue, job, t):
-                k, a0, na = job
+            def store(queue, k, a0, na, t):
                 n, q = k // 4, k % 4
                 queue.dma_start(
                     out=out_v[:, NB * n + a0 : NB * n + a0 + na, QO * q : QO * (q + 1)], in_=t[:, 0:na, :]
                 )
 
-            def tapsum_pe(job):
-                npair = job[2] // 2
-                flat = prod[job][:].rearrange("p a f -> p (a f)")
+            def tapsum_pe(k, last):
+                flat = prod[k][:].rearrange("p a f -> p (a f)")
                 acc = ps_a.tile([P, NB // 2, P], F32, name="acc", tag="a")
-                for r in range(npair):
+                for r in range(NB // 2):
                     for m in range(TAPS):
                         f0 = 2 * QF * r + m
                         nc.tensor.matmul(
@@ -349,68 +342,54 @@ def tile_involution2d_pa_kernel(tc, x_bytes, x_scale, Wi, bi, w_span, out):
                             start=(m == 0),
                             stop=(m == TAPS - 1),
                         )
+                    if r == 0 and last is not None:
+                        back(last)
                 t = ot_pool.tile([P, NB // 2, P], F32, name="o_t", tag="o_t")
-                nc.scalar.copy(out=t[:, 0:npair, :], in_=acc[:, 0:npair, :])
-                o_t[job] = t
+                nc.scalar.copy(out=t[:], in_=acc[:])
+                o_t[k] = t
 
-            def back(job):
-                na = job[2]
-                npair = na // 2
+            def back(k):
                 ob = ps_b.tile([P, NB // 2, P], F32, name="ob", tag="b")
-                for r in range(npair):
-                    nc.tensor.transpose(ob[:, r, :], o_t[job][:, r, :], ident[:])
+                for r in range(NB // 2):
+                    nc.tensor.transpose(ob[:, r, :], o_t[k][:, r, :], ident[:])
                 t = osb_pool.tile([P, NB, QO], F32, name="osb", tag="osb")
-                nc.scalar.copy(
-                    out=t[:, 0:na, :].rearrange("p a o -> p (a o)"), in_=ob[:, 0:npair, :].rearrange("p r c -> p (r c)")
-                )
-                store(nc.scalar, job, t)
+                nc.scalar.copy(out=t[:].rearrange("p a o -> p (a o)"), in_=ob[:].rearrange("p r c -> p (r c)"))
+                store(nc.scalar, k, 0, NB, t)
 
-            def tapsum_v(job, step):
-                k, a0, na = job
-                pv = prod[job][:].rearrange("p a (o m) -> p a o m", m=TAPS)
-                for a in range(0, na, step):
+            def tapsum_v(k, step):
+                pv = prod[k][:].rearrange("p a (o m) -> p a o m", m=TAPS)
+                for a in range(0, NB, step):
                     t = osb_pool.tile([P, NB, QO], F32, name="osv", tag="osv")
                     nc.vector.tensor_reduce(
                         out=t[:, 0:step, :], in_=pv[:, a : a + step], axis=mybir.AxisListType.X, op=ADD
                     )
-                    store(nc.sync, (k, a0 + a, step), t)
+                    store(nc.sync, k, a, step, t)
 
-            ticks = []
-            for i in range(len(V_JOBS)):
-                ticks.append(("mult", i))
-                if V_JOBS[i] in V_SUM:
-                    ticks.append(("sum", i))
-            for job in G_JOBS[0:3]:
-                mult("g", job)
-            pend = []
-            for tick in range(len(ticks) + 2):
-                todo = []
-                if tick < len(ticks):
-                    what, i = ticks[tick]
-                    job = V_JOBS[i]
-                    if what == "sum":
-                        if i == len(V_JOBS) - 1:
-                            tapsum_v(job, 2)
-                        else:
-                            tapsum_v(job, job[2])
-                    else:
-                        mult("v", job)
-                        if i + 3 < len(V_JOBS) and V_JOBS[i + 3][0] not in wps:
-                            rows("v", V_JOBS[i + 3][0])
-                            wcopy(V_JOBS[i + 3][0])
-                        if job not in V_SUM:
-                            todo.append(job)
-                for job in pend:
-                    back(job)
-                for i in range(len(G_JOBS)):
-                    if G_AFTER[i] == tick:
-                        todo.append(G_JOBS[i])
-                for job in todo:
-                    tapsum_pe(job)
-                    if job in G_JOBS and G_JOBS.index(job) + 3 < len(G_JOBS):
-                        nxt = G_JOBS[G_JOBS.index(job) + 3]
-                        rows("g", nxt[0])
+            ph2.enter_context(
+                tc.manual_schedule(
+                    engines={mybir.EngineType.PE, mybir.EngineType.DVE, mybir.EngineType.Activation, mybir.EngineType.SP}
+                )
+            )
+            sums = list(PE_ORDER)
+            last = None
+            for k in G_UNITS[0:3]:
+                mult("g", k)
+            for i in range(len(V_UNITS)):
+                k = V_UNITS[i]
+                mult("v", k)
+                if i + 2 < len(V_UNITS):
+                    rows("v", V_UNITS[i + 2])
+                    wcopy(V_UNITS[i + 2])
+                if k in V_SUM:
+                    tapsum_v(k, 2 if i == len(V_UNITS) - 1 else NB)
+                while sums and sums[0] in prod:
+                    nxt = sums.pop(0)
+                    tapsum_pe(nxt, last)
+                    last = nxt
+                    if nxt in G_UNITS and G_UNITS.index(nxt) + 3 < len(G_UNITS):
+                        nxt = G_UNITS[G_UNITS.index(nxt) + 3]
+                        rows("g", nxt)
                         mult("g", nxt)
-                pend = todo
-            for job in pend:
-                back(job)
+                    if sums and sums[0] in G_UNITS and i + 1 < len(V_UNITS):
+                        break
+            back(last)

@@ -25,6 +25,7 @@ ROW3 = 768
 QO = 64
 QF = QO * TAPS
 NB = 8
+OV = QO + 4
 NCH = NV // 2
 WCOL = 45
 G_UNITS = (0, 1, 2, 3, 4, 5)
@@ -356,14 +357,16 @@ def tile_involution2d_pa_kernel(tc, x_bytes, x_scale, Wi, bi, w_span, out):
                 nc.scalar.copy(out=t[:].rearrange("p a o -> p (a o)"), in_=ob[:].rearrange("p r c -> p (r c)"))
                 store(nc.scalar, k, 0, NB, t)
 
-            def tapsum_v(k, step):
+            def tapsum_v(k, cuts):
                 pv = prod[k][:].rearrange("p a (o m) -> p a o m", m=TAPS)
-                for a in range(0, NB, step):
-                    t = osb_pool.tile([P, NB, QO], F32, name="osv", tag="osv")
+                a = 0
+                for n in cuts:
+                    t = osb_pool.tile([P, NB, OV], F32, name="osv", tag="osv")
                     nc.vector.tensor_reduce(
-                        out=t[:, 0:step, :], in_=pv[:, a : a + step], axis=mybir.AxisListType.X, op=ADD
+                        out=t[:, 0:n, 0:QO], in_=pv[:, a : a + n], axis=mybir.AxisListType.X, op=ADD
                     )
-                    store(nc.sync, k, a, step, t)
+                    store(nc.sync, k, a, n, t[:, :, 0:QO])
+                    a += n
 
             ph2.enter_context(
                 tc.manual_schedule(
@@ -381,7 +384,7 @@ def tile_involution2d_pa_kernel(tc, x_bytes, x_scale, Wi, bi, w_span, out):
                     rows("v", V_UNITS[i + 2])
                     wcopy(V_UNITS[i + 2])
                 if k in V_SUM:
-                    tapsum_v(k, 2 if i == len(V_UNITS) - 1 else NB)
+                    tapsum_v(k, (3, 3, 1, 1) if i == len(V_UNITS) - 1 else (5, 3))
                 while sums and sums[0] in prod:
                     nxt = sums.pop(0)
                     tapsum_pe(nxt, last)

@@ -28,10 +28,13 @@ NB = 8
 OV = QO + 4
 NCH = NV // 2
 WCOL = 45
-G_UNITS = (0, 1, 2, 3, 4, 5)
-V_UNITS = (6, 7, 8, 9, 10, 11, 12, 13, 14, 15)
-V_SUM = (8, 10, 12, 13, 14, 15)
-PE_ORDER = (6, 7, 0, 9, 1, 11, 2, 3, 4, 5)
+G_JOBS = ((0, 0, 8), (1, 0, 8), (2, 0, 8), (3, 4, 4), (4, 0, 8), (5, 0, 8), (7, 0, 4))
+S_JOB = (3, 0, 4)
+S_PART = 6
+G_BUFS = 3
+V_JOBS = ((7, 4, 4), (6, 0, 8), (8, 0, 8), (9, 0, 8), (10, 0, 8), (11, 0, 8), (12, 0, 8), (13, 0, 8), (14, 0, 8), (15, 0, 8))
+V_SUM = (2, 4, 6, 7, 8, 9)
+PE_ORDER = (("v", 0), ("v", 1), ("g", 0), ("v", 3), ("g", 1), ("v", 5), ("g", 2), ("g", 3), ("s", 0), ("g", 4), ("g", 5), ("g", 6))
 
 
 def pieces(q):
@@ -83,8 +86,8 @@ def tile_involution2d_pa_kernel(tc, x_bytes, x_scale, Wi, bi, w_span, out):
         const = ctx.enter_context(tc.tile_pool(name="const", bufs=1))
         prod_pool = ctx.enter_context(tc.tile_pool(name="prodp", bufs=3))
         xsh_pool = ctx.enter_context(tc.tile_pool(name="xshp", bufs=2))
-        ot_pool = ctx.enter_context(tc.tile_pool(name="otp", bufs=4))
-        osb_pool = ctx.enter_context(tc.tile_pool(name="osbp", bufs=4))
+        ot_pool = ctx.enter_context(tc.tile_pool(name="otp", bufs=3))
+        osb_pool = ctx.enter_context(tc.tile_pool(name="osbp", bufs=3))
         ps_a = ctx.enter_context(tc.psum_pool(name="psa", bufs=4))
         ps_b = ctx.enter_context(tc.psum_pool(name="psb", bufs=1))
         ps_w = ctx.enter_context(tc.psum_pool(name="psw", bufs=3))
@@ -118,12 +121,9 @@ def tile_involution2d_pa_kernel(tc, x_bytes, x_scale, Wi, bi, w_span, out):
         xs1 = const.tile([P, 35 * F], F32, name="xs1", tag="xs1")
         nc.gpsimd.memset(xs1[:, 0:F], 0.0)
         nc.gpsimd.memset(xs1[:, 33 * F : 34 * F], 0.0)
-        g_units = G_UNITS
+        g_units = tuple(job[0] for job in G_JOBS)
         for k in g_units:
             wsb[k] = const.tile([P, NB, WCOL], F32, name="wsb%d" % k, tag="wsb%d" % k)
-        xit = []
-        for j in range(3):
-            xit.append(const.tile([P, 2, F], F32, name="xit%d" % j, tag="xit%d" % j))
         wi_codes = const.tile([P, 2 * F], U32, name="wi_codes", tag="wi_codes", align_bytes=64)
         wi_sc = const.tile([P, 2 * F], U8, name="wi_sc", tag="wi_sc", align_bytes=64)
 
@@ -170,11 +170,17 @@ def tile_involution2d_pa_kernel(tc, x_bytes, x_scale, Wi, bi, w_span, out):
             else:
                 nc.sync.dma_start(out=dst[P - 1 : P, 0 : 10 * F], in_=xs1[0:1, cols])
 
+        ctx.enter_context(tc.manual_schedule(engines={mybir.EngineType.Pool}))
+
         with ExitStack() as ph1:
             c1 = ph1.enter_context(tc.tile_pool(name="c1", bufs=1))
             bytes_pool = ph1.enter_context(tc.tile_pool(name="bytes", bufs=2))
             xbf_pool = ph1.enter_context(tc.tile_pool(name="xbfp", bufs=3))
             grp_pool = ph1.enter_context(tc.tile_pool(name="grpp", bufs=3))
+            xit_pool = ph1.enter_context(tc.tile_pool(name="xitp", bufs=1))
+            xit = []
+            for j in range(3):
+                xit.append(xit_pool.tile([P, 2, F], F32, name="xit%d" % j, tag="xit%d" % j))
 
             def load(q, parts):
                 t = bytes_pool.tile([P, 4 * C], U8, name="xb", tag="xb")
@@ -229,6 +235,8 @@ def tile_involution2d_pa_kernel(tc, x_bytes, x_scale, Wi, bi, w_span, out):
 
             def quant_mm(c):
                 codes = grp_pool.tile([P, 512], U32, name="codes", tag="codes", align_bytes=64)
+                if c == NCH - 1:
+                    last_codes.append(codes)
                 sc = grp_pool.tile([P, 512], U8, name="sc", tag="sc", align_bytes=64)
                 nc.vector.quantize_mx(out=codes[:].bitcast(FP8X4), scales=sc[:], in_=grp[c][:])
                 mmp = ps_b.tile([P, 2, F], F32, name="mmp", tag="b")
@@ -263,7 +271,8 @@ def tile_involution2d_pa_kernel(tc, x_bytes, x_scale, Wi, bi, w_span, out):
                         )
                 nc.scalar.copy(out=xs1[:, F * (1 + 2 * c) : F * (3 + 2 * c)], in_=pt[:].rearrange("p a c -> p (a c)"))
 
-            early = [("g", k) for k in g_units[0:4]] + [("v", k) for k in V_UNITS[0:3]]
+            last_codes = []
+            early = [("g", k) for k in g_units[0:4]] + [("v", job[0]) for job in V_JOBS[0:3]]
             for t in range(NCH + 3):
                 if t < NCH:
                     widen(t)
@@ -281,63 +290,94 @@ def tile_involution2d_pa_kernel(tc, x_bytes, x_scale, Wi, bi, w_span, out):
                 if 3 <= t < 3 + len(g_units):
                     wmask(g_units[t - 3])
                 if t == 3 + len(g_units):
-                    for k in V_UNITS[0:2]:
-                        wcopy(k)
+                    for job in V_JOBS[0:2]:
+                        wcopy(job[0])
+
+            mark = const.tile([P, 1], U32, name="mark", tag="mark")
+            nc.gpsimd.tensor_copy(out=mark[:], in_=last_codes[0][:, 0:1])
 
         with ExitStack() as ph2:
-            gm_pool = ph2.enter_context(tc.tile_pool(name="gmp", bufs=3, reuse_waits="tile"))
+            gm_pool = ph2.enter_context(tc.tile_pool(name="gmp", bufs=G_BUFS, reuse_waits="tile"))
 
-            def source(who, k, lo, ln):
+            def source(who, job, lo, ln):
+                k, a0, na = job
                 i = lo // ROW3
                 if i == 1:
                     src, st = xs1, F * NB * (k // 4) + lo - ROW3
                 else:
                     src, st = xsh[(who, k // 4, i // 2)], lo - ROW3 * i
-                return src[:, st : st + F * NB].rearrange("p (a c) -> p a c", c=F)[:, :, 0:ln]
+                return src[:, st : st + F * NB].rearrange("p (a c) -> p a c", c=F)[:, a0 : a0 + na, 0:ln]
 
-            def mult(who, k):
+            def mult(who, job):
+                k, a0, na = job
                 q = k % 4
                 if who == "v":
                     eng = nc.vector
                     pd = prod_pool.tile([P, NB, QF], F32, name="pd", tag="pd", align_bytes=64)
-                    wk = wps[k]
+                    wk = wps[k][:, a0 : a0 + na]
                 else:
                     eng = nc.gpsimd
                     pd = gm_pool.tile([P, NB, QF], F32, name="gm", tag="gm")
-                    wk = wsb[k]
-                prod[k] = pd
+                    wk = wsb[k][:, a0 : a0 + na]
+                prod[job] = pd
                 for lo, hi, whole in pieces(q):
                     ln = hi - lo
-                    win = source(who, k, lo, ln)
-                    dst = pd[:, :, lo - QF * q : hi - QF * q]
+                    win = source(who, job, lo, ln)
+                    dst = pd[:, 0:na, lo - QF * q : hi - QF * q]
                     w0 = TAPS * blocks(q).index((lo // GRP, lo // ROW3))
                     if whole:
-                        nj = ln // TAPS
                         eng.tensor_tensor(
                             out=dst.rearrange("p a (j m) -> p a j m", m=TAPS),
                             in0=win.rearrange("p a (j m) -> p a j m", m=TAPS),
-                            in1=wk[:, :, w0 : w0 + TAPS].unsqueeze(2).to_broadcast([P, NB, nj, TAPS]),
+                            in1=wk[:, :, w0 : w0 + TAPS].unsqueeze(2).to_broadcast([P, na, ln // TAPS, TAPS]),
                             op=MULT,
                         )
                     else:
                         m0 = lo % TAPS
                         eng.tensor_tensor(out=dst, in0=win, in1=wk[:, :, w0 + m0 : w0 + m0 + ln], op=MULT)
 
-            def store(queue, k, a0, na, t):
-                n, q = k // 4, k % 4
-                queue.dma_start(
-                    out=out_v[:, NB * n + a0 : NB * n + a0 + na, QO * q : QO * (q + 1)], in_=t[:, 0:na, :]
-                )
+            def small_products(job):
+                k, a0, na = job
+                q = k % 4
+                pd = gm_pool.tile([P, TAPS, na, QO], F32, name="sm", tag="sm", bufs=1)
+                prod[job] = pd
+                steps = []
+                for lo, hi, whole in pieces(q):
+                    w0 = TAPS * blocks(q).index((lo // GRP, lo // ROW3))
+                    win = source("g", job, lo, hi - lo)
+                    o0 = (lo - QF * q) // TAPS
+                    for a in range(na):
+                        for m in range(TAPS):
+                            steps.append(
+                                (
+                                    pd[:, m, a, o0 : o0 + (hi - lo) // TAPS],
+                                    win[:, a, m : hi - lo : TAPS],
+                                    wsb[k][:, a0 + a, w0 + m : w0 + m + 1],
+                                )
+                            )
+                return steps
 
-            def tapsum_pe(k, last):
-                flat = prod[k][:].rearrange("p a f -> p (a f)")
+            def store(queue, job, a, na, t):
+                k = job[0]
+                n, q = k // 4, k % 4
+                v0 = NB * n + job[1] + a
+                queue.dma_start(out=out_v[:, v0 : v0 + na, QO * q : QO * (q + 1)], in_=t[:, 0:na, :])
+
+            def tap(job, r, m):
+                if job == S_JOB:
+                    n = job[2] * QO
+                    return prod[job][:].rearrange("p m a o -> p (m a o)")[:, n * m + P * r : n * m + P * (r + 1)]
+                f0 = 2 * QF * r + m
+                return prod[job][:].rearrange("p a f -> p (a f)")[:, f0 : f0 + TAPS * (P - 1) + 1 : TAPS]
+
+            def tapsum_pe(job, last):
+                npair = job[2] // 2
                 acc = ps_a.tile([P, NB // 2, P], F32, name="acc", tag="a")
-                for r in range(NB // 2):
+                for r in range(npair):
                     for m in range(TAPS):
-                        f0 = 2 * QF * r + m
                         nc.tensor.matmul(
                             out=acc[:, r, :],
-                            lhsT=flat[:, f0 : f0 + TAPS * (P - 1) + 1 : TAPS],
+                            lhsT=tap(job, r, m),
                             rhs=ident[:],
                             is_transpose=True,
                             start=(m == 0),
@@ -346,26 +386,30 @@ def tile_involution2d_pa_kernel(tc, x_bytes, x_scale, Wi, bi, w_span, out):
                     if r == 0 and last is not None:
                         back(last)
                 t = ot_pool.tile([P, NB // 2, P], F32, name="o_t", tag="o_t")
-                nc.scalar.copy(out=t[:], in_=acc[:])
-                o_t[k] = t
+                nc.scalar.copy(out=t[:, 0:npair, :], in_=acc[:, 0:npair, :])
+                o_t[job] = t
 
-            def back(k):
+            def back(job):
+                npair = job[2] // 2
                 ob = ps_b.tile([P, NB // 2, P], F32, name="ob", tag="b")
-                for r in range(NB // 2):
-                    nc.tensor.transpose(ob[:, r, :], o_t[k][:, r, :], ident[:])
+                for r in range(npair):
+                    nc.tensor.transpose(ob[:, r, :], o_t[job][:, r, :], ident[:])
                 t = osb_pool.tile([P, NB, QO], F32, name="osb", tag="osb")
-                nc.scalar.copy(out=t[:].rearrange("p a o -> p (a o)"), in_=ob[:].rearrange("p r c -> p (r c)"))
-                store(nc.scalar, k, 0, NB, t)
+                nc.scalar.copy(
+                    out=t[:, 0 : job[2], :].rearrange("p a o -> p (a o)"),
+                    in_=ob[:, 0:npair, :].rearrange("p r c -> p (r c)"),
+                )
+                store(nc.scalar, job, 0, job[2], t)
 
-            def tapsum_v(k, cuts):
-                pv = prod[k][:].rearrange("p a (o m) -> p a o m", m=TAPS)
+            def tapsum_v(job, cuts):
+                pv = prod[job][:].rearrange("p a (o m) -> p a o m", m=TAPS)
                 a = 0
                 for n in cuts:
                     t = osb_pool.tile([P, NB, OV], F32, name="osv", tag="osv")
                     nc.vector.tensor_reduce(
                         out=t[:, 0:n, 0:QO], in_=pv[:, a : a + n], axis=mybir.AxisListType.X, op=ADD
                     )
-                    store(nc.sync, k, a, n, t[:, :, 0:QO])
+                    store(nc.sync, job, a, n, t[:, :, 0:QO])
                     a += n
 
             ph2.enter_context(
@@ -373,26 +417,36 @@ def tile_involution2d_pa_kernel(tc, x_bytes, x_scale, Wi, bi, w_span, out):
                     engines={mybir.EngineType.PE, mybir.EngineType.DVE, mybir.EngineType.Activation, mybir.EngineType.SP}
                 )
             )
-            sums = list(PE_ORDER)
-            last = None
-            for k in G_UNITS[0:3]:
-                mult("g", k)
-            for i in range(len(V_UNITS)):
-                k = V_UNITS[i]
-                mult("v", k)
-                if i + 2 < len(V_UNITS):
-                    rows("v", V_UNITS[i + 2])
-                    wcopy(V_UNITS[i + 2])
-                if k in V_SUM:
-                    tapsum_v(k, (3, 3, 1, 1) if i == len(V_UNITS) - 1 else (5, 3))
+            jobs = {"v": V_JOBS, "g": G_JOBS, "s": (S_JOB,)}
+            sums = [jobs[who][i] for who, i in PE_ORDER]
+            small = small_products(S_JOB)
+            share = -(-len(small) // S_PART)
+            done = []
+            for job in G_JOBS[0:G_BUFS]:
+                mult("g", job)
+            for i in range(len(V_JOBS)):
+                job = V_JOBS[i]
+                mult("v", job)
+                if i + 2 < len(V_JOBS):
+                    rows("v", V_JOBS[i + 2][0])
+                    wcopy(V_JOBS[i + 2][0])
+                if i in V_SUM:
+                    tapsum_v(job, (3, 3, 1, 1) if i == len(V_JOBS) - 1 else (5, 3))
                 while sums and sums[0] in prod:
-                    nxt = sums.pop(0)
-                    tapsum_pe(nxt, last)
-                    last = nxt
-                    if nxt in G_UNITS and G_UNITS.index(nxt) + 3 < len(G_UNITS):
-                        nxt = G_UNITS[G_UNITS.index(nxt) + 3]
-                        rows("g", nxt)
+                    job = sums.pop(0)
+                    while job == S_JOB and small:
+                        dst, src, w = small.pop(0)
+                        nc.scalar.activation(out=dst, in_=src, func=ACT.Copy, scale=w)
+                    tapsum_pe(job, done[-1] if done else None)
+                    done.append(job)
+                    for n in range(share):
+                        if small:
+                            dst, src, w = small.pop(0)
+                            nc.scalar.activation(out=dst, in_=src, func=ACT.Copy, scale=w)
+                    if job in G_JOBS and G_JOBS.index(job) + G_BUFS < len(G_JOBS):
+                        nxt = G_JOBS[G_JOBS.index(job) + G_BUFS]
+                        rows("g", nxt[0])
                         mult("g", nxt)
-                    if sums and sums[0] in G_UNITS and i + 1 < len(V_UNITS):
+                    if sums and sums[0] in G_JOBS and i + 1 < len(V_JOBS):
                         break
-            back(last)
+            back(done[-1])

from contextlib import ExitStack

import concourse.mybir as mybir
from concourse.masks import make_identity

FLOPS = 2 * 4096 * 1024 * 256 + 2 * 4096 * 256 * 9

F32 = mybir.dt.float32
BF16 = mybir.dt.bfloat16
U32 = mybir.dt.uint32
U8 = mybir.dt.uint8
FP8 = mybir.dt.float8_e4m3fn
FP8X4 = mybir.dt.float8_e4m3fn_x4
MULT = mybir.AluOpType.mult
ADD = mybir.AluOpType.add
ACT = mybir.ActivationFunctionType

P = 128
NV = 32
C = 1024
F = 256
TAPS = 9
GRP = 144
ROW3 = 768
QO = 64
QF = QO * TAPS
NB = 8
OV = QO + 4
NCH = NV // 2
WCOL = 45
G_JOBS = ((0, 0, 8), (1, 0, 8), (2, 0, 8), (3, 4, 4), (4, 0, 8), (5, 0, 8), (7, 0, 4))
S_JOB = (3, 0, 4)
S_PART = 6
G_BUFS = 3
V_JOBS = ((7, 4, 4), (6, 0, 8), (8, 0, 8), (9, 0, 8), (10, 0, 8), (11, 0, 8), (12, 0, 8), (13, 0, 8), (14, 0, 8), (15, 0, 8))
V_SUM = (2, 4, 6, 7, 8, 9)
PE_ORDER = (("v", 0), ("v", 1), ("g", 0), ("v", 3), ("g", 1), ("v", 5), ("g", 2), ("g", 3), ("s", 0), ("g", 4), ("g", 5), ("g", 6))


def pieces(q):
    res = []
    f = QF * q
    end = QF * (q + 1)
    while f < end:
        nxt = min(end, (f // GRP + 1) * GRP, (f // ROW3 + 1) * ROW3)
        lo = f
        if lo % TAPS:
            e = min(nxt, lo + TAPS - lo % TAPS)
            res.append((lo, e, False))
            lo = e
        body = nxt - (nxt - lo) % TAPS
        if body > lo:
            res.append((lo, body, True))
        if nxt > body:
            res.append((body, nxt, False))
        f = nxt
    return res


def blocks(q):
    res = []
    for lo, hi, whole in pieces(q):
        pair = (lo // GRP, lo // ROW3)
        if pair not in res:
            res.append(pair)
    return res


def runs(q):
    res = []
    for b, (g, i) in enumerate(blocks(q)):
        if res and res[-1][0] == i:
            res[-1] = (i, res[-1][1], res[-1][2] + 1, res[-1][3])
        else:
            res.append((i, b, 1, g))
    return res


def tile_involution2d_pa_kernel(tc, x_bytes, x_scale, Wi, bi, w_span, out):
    nc = tc.nc
    xb_v = x_bytes.rearrange("b u v k -> (b u) (v k)")
    w_v = w_span.rearrange("b u v c -> (b u) (v c)")
    out_v = out.rearrange("b u v o -> (b u) v o")

    with ExitStack() as ctx:
        const = ctx.enter_context(tc.tile_pool(name="const", bufs=1))
        prod_pool = ctx.enter_context(tc.tile_pool(name="prodp", bufs=3))
        xsh_pool = ctx.enter_context(tc.tile_pool(name="xshp", bufs=2))
        ot_pool = ctx.enter_context(tc.tile_pool(name="otp", bufs=3))
        osb_pool = ctx.enter_context(tc.tile_pool(name="osbp", bufs=3))
        ps_a = ctx.enter_context(tc.psum_pool(name="psa", bufs=4))
        ps_b = ctx.enter_context(tc.psum_pool(name="psb", bufs=1))
        ps_w = ctx.enter_context(tc.psum_pool(name="psw", bufs=3))

        xb = {}
        xbf = {}
        grp = {}
        prod = {}
        o_t = {}
        wps = {}
        wsb = {}
        xsh = {}

        w_t = const.tile([P, NV, GRP], BF16, name="w_t", tag="w_t")
        bias_t = const.tile([P, 2], BF16, name="bias_t", tag="bias_t")
        ident = const.tile([P, P], F32, name="ident", tag="ident")
        make_identity(nc, ident[:])
        ident_bf = const.tile([P, P], BF16, name="ident_bf", tag="ident_bf")
        make_identity(nc, ident_bf[:])
        ind = const.tile([P, 2], F32, name="ind", tag="ind")
        nc.vector.tensor_reduce(out=ind[:, 0:1], in_=ident[:, 0:P:32], axis=mybir.AxisListType.X, op=ADD)
        nc.vector.tensor_reduce(out=ind[:, 1:2], in_=ident[:, 31:P:32], axis=mybir.AxisListType.X, op=ADD)
        edge = const.tile([P, 2], F32, name="edge", tag="edge")
        nc.vector.tensor_scalar(out=edge[:], in0=ind[:], scalar1=-1.0, scalar2=1.0, op0=MULT, op1=ADD)
        dg = []
        for e in range(2):
            t = const.tile([P, P], BF16, name="dg%d" % e, tag="dg%d" % e)
            nc.vector.tensor_scalar_mul(out=t[:], in0=ident_bf[:], scalar1=edge[:, e : e + 1])
            dg.append(t)
        wdiag = (dg[0], ident_bf, dg[1])
        xs1 = const.tile([P, 35 * F], F32, name="xs1", tag="xs1")
        nc.gpsimd.memset(xs1[:, 0:F], 0.0)
        nc.gpsimd.memset(xs1[:, 33 * F : 34 * F], 0.0)
        g_units = tuple(job[0] for job in G_JOBS)
        for k in g_units:
            wsb[k] = const.tile([P, NB, WCOL], F32, name="wsb%d" % k, tag="wsb%d" % k)
        wi_codes = const.tile([P, 2 * F], U32, name="wi_codes", tag="wi_codes", align_bytes=64)
        wi_sc = const.tile([P, 2 * F], U8, name="wi_sc", tag="wi_sc", align_bytes=64)

        def wcopy(k):
            n, q = k // 4, k % 4
            t = ps_w.tile([P, NB, WCOL], F32, name="wps", tag="wps")
            for i, b0, nb, g0 in runs(q):
                nc.tensor.matmul(
                    out=t[:, :, TAPS * b0 : TAPS * (b0 + nb)],
                    lhsT=wdiag[i][:],
                    rhs=w_t[:, NB * n : NB * (n + 1), TAPS * g0 : TAPS * (g0 + nb)],
                    start=True,
                    stop=True,
                )
            wps[k] = t

        def wmask(k):
            n, q = k // 4, k % 4
            for i, b0, nb, g0 in runs(q):
                src = w_t[:, NB * n : NB * (n + 1), TAPS * g0 : TAPS * (g0 + nb)]
                dst = wsb[k][:, :, TAPS * b0 : TAPS * (b0 + nb)]
                if i == 1:
                    nc.scalar.copy(out=dst, in_=src)
                else:
                    nc.scalar.activation(out=dst, in_=src, func=ACT.Copy, scale=edge[:, i // 2 : i // 2 + 1])

        def rows(who, k):
            n, d = k // 4, k % 4 // 2
            if (who, n, d) in xsh:
                return
            if who == "g":
                dst = xsh_pool.tile([P, 11 * F], F32, name="xshg", tag="xshg")
            else:
                dst = xsh_pool.tile([P, 11 * F], F32, name="xshv", tag="xshv")
            xsh[(who, n, d)] = dst
            cols = slice(F * NB * n, F * (NB * n + 10))
            for lo, hi in ((0, 112), (112, 127)):
                if d == 0:
                    nc.sync.dma_start(out=dst[lo + 1 : hi + 1, 0 : 10 * F], in_=xs1[lo:hi, cols])
                else:
                    nc.sync.dma_start(out=dst[lo:hi, 0 : 10 * F], in_=xs1[lo + 1 : hi + 1, cols])
            if d == 0:
                nc.sync.dma_start(out=dst[0:1, 0 : 10 * F], in_=xs1[P - 1 : P, cols])
            else:
                nc.sync.dma_start(out=dst[P - 1 : P, 0 : 10 * F], in_=xs1[0:1, cols])

        ctx.enter_context(tc.manual_schedule(engines={mybir.EngineType.Pool}))

        with ExitStack() as ph1:
            c1 = ph1.enter_context(tc.tile_pool(name="c1", bufs=1))
            bytes_pool = ph1.enter_context(tc.tile_pool(name="bytes", bufs=2))
            xbf_pool = ph1.enter_context(tc.tile_pool(name="xbfp", bufs=3))
            grp_pool = ph1.enter_context(tc.tile_pool(name="grpp", bufs=3))
            xit_pool = ph1.enter_context(tc.tile_pool(name="xitp", bufs=1))
            xit = []
            for j in range(3):
                xit.append(xit_pool.tile([P, 2, F], F32, name="xit%d" % j, tag="xit%d" % j))

            def load(q, parts):
                t = bytes_pool.tile([P, 4 * C], U8, name="xb", tag="xb")
                w = 4 * C // parts
                for s in range(parts):
                    nc.sync.dma_start(
                        out=t[:, w * s : w * (s + 1)], in_=xb_v[:, 4 * C * q + w * s : 4 * C * q + w * (s + 1)]
                    )
                xb[q] = t

            scale_bc = c1.tile([P, 2 * C], F32, name="scale_bc", tag="scale_bc")
            nc.scalar.dma_start(
                out=scale_bc[:, 0:C], in_=x_scale.rearrange("a b c k -> (a b c k)").partition_broadcast(P)
            )
            load(0, 4)
            wi_raw = prod_pool.tile([P, 2, 4, F], BF16, name="wi_raw", tag="pd", align_bytes=64)
            nc.sync.dma_start(out=wi_raw[:], in_=Wi.rearrange("(g p t) n -> p g t n", p=P, t=4))
            with nc.allow_non_contiguous_dma(reason="256 bias values, one to a partition"):
                nc.sync.dma_start(out=bias_t[:], in_=bi.rearrange("(h p) -> p h", p=P))
            load(1, 1)
            nc.sync.dma_start(out=w_t[:].rearrange("p v c -> p (v c)"), in_=w_v)

            nc.scalar.copy(out=scale_bc[:, C : 2 * C], in_=scale_bc[:, 0:C])
            wi_grp = prod_pool.tile([P, 2, F, 4], BF16, name="wi_grp", tag="pd", align_bytes=64)
            nc.scalar.copy(out=wi_grp[:], in_=wi_raw[:].rearrange("p g t n -> p g n t"))
            nc.vector.quantize_mx(
                out=wi_codes[:].bitcast(FP8X4), scales=wi_sc[:], in_=wi_grp[:].rearrange("p g n t -> p (g n t)")
            )

            def widen(c):
                t = xbf_pool.tile([P, 2 * C], BF16, name="xbf", tag="xbf")
                xbf[c] = t
                src = xb[c // 2][:, 2 * C * (c % 2) : 2 * C * (c % 2 + 1)].bitcast(FP8)
                if c == 0:
                    for vl in range(2):
                        cols = slice(C * vl, C * (vl + 1))
                        nc.vector.tensor_tensor(out=t[:, cols], in0=src[:, cols], in1=scale_bc[:, 0:C], op=MULT)
                else:
                    nc.vector.tensor_tensor(out=t[:], in0=src, in1=scale_bc[:], op=MULT)

            def xpose(c):
                g_t = grp_pool.tile([P, 2048], BF16, name="grp", tag="grp", align_bytes=64)
                grp[c] = g_t
                gw = g_t[:].bitcast(F32).rearrange("p (g r u) -> p g r u", g=2, u=2)
                for vl in range(2):
                    words = xbf[c][:, C * vl : C * (vl + 1)].bitcast(F32)
                    xt = ps_a.tile([P, 2, 2, P], F32, name="xt", tag="a")
                    for g in range(2):
                        for u in range(2):
                            nc.tensor.transpose(xt[:, g, u, :], words[:, 256 * g + u : 256 * (g + 1) : 2], ident[:])
                    nc.scalar.copy(out=gw[:, :, P * vl : P * (vl + 1), :], in_=xt[:].rearrange("p g u r -> p g r u"))

            def quant_mm(c):
                codes = grp_pool.tile([P, 512], U32, name="codes", tag="codes", align_bytes=64)
                if c == NCH - 1:
                    last_codes.append(codes)
                sc = grp_pool.tile([P, 512], U8, name="sc", tag="sc", align_bytes=64)
                nc.vector.quantize_mx(out=codes[:].bitcast(FP8X4), scales=sc[:], in_=grp[c][:])
                mmp = ps_b.tile([P, 2, F], F32, name="mmp", tag="b")
                for h in range(2):
                    for g in range(2):
                        wcols = slice(F * g + P * h, F * g + P * (h + 1))
                        xcols = slice(F * g, F * (g + 1))
                        nc.tensor.matmul_mx(
                            out=mmp[:, h, :],
                            lhsT=wi_codes[:, wcols].bitcast(FP8X4),
                            lhsT_scale=wi_sc[:, wcols],
                            rhs=codes[:, xcols].bitcast(FP8X4),
                            rhs_scale=sc[:, xcols],
                            start=(g == 0),
                            stop=(g == 1),
                        )
                for h in range(2):
                    nc.scalar.activation(
                        out=xit[c % 3][:, h, :],
                        in_=mmp[:, h, :],
                        func=ACT.Identity,
                        bias=bias_t[:, h : h + 1],
                        scale=1.0,
                    )

            def turn(c):
                pt = ps_a.tile([P, 2, F], F32, name="pt", tag="a")
                for vl in range(2):
                    for h in range(2):
                        nc.tensor.transpose(
                            pt[:, vl, P * h : P * (h + 1)], xit[c % 3][:, h, P * vl : P * (vl + 1)], ident[:]
                        )
                nc.scalar.copy(out=xs1[:, F * (1 + 2 * c) : F * (3 + 2 * c)], in_=pt[:].rearrange("p a c -> p (a c)"))

            last_codes = []
            early = [("g", k) for k in g_units[0:4]] + [("v", job[0]) for job in V_JOBS[0:3]]
            for t in range(NCH + 3):
                if t < NCH:
                    widen(t)
                    xpose(t)
                if t % 2 == 1 and t // 2 + 2 < NV // 4:
                    load(t // 2 + 2, 1)
                if 0 <= t - 2 < NCH:
                    quant_mm(t - 2)
                if 0 <= t - 3 < NCH:
                    c = t - 3
                    turn(c)
                    for who, k in early:
                        if c == min(k // 4 * 4 + 4, NCH - 1):
                            rows(who, k)
                if 3 <= t < 3 + len(g_units):
                    wmask(g_units[t - 3])
                if t == 3 + len(g_units):
                    for job in V_JOBS[0:2]:
                        wcopy(job[0])

            mark = const.tile([P, 1], U32, name="mark", tag="mark")
            nc.gpsimd.tensor_copy(out=mark[:], in_=last_codes[0][:, 0:1])

        with ExitStack() as ph2:
            gm_pool = ph2.enter_context(tc.tile_pool(name="gmp", bufs=G_BUFS, reuse_waits="tile"))

            def source(who, job, lo, ln):
                k, a0, na = job
                i = lo // ROW3
                if i == 1:
                    src, st = xs1, F * NB * (k // 4) + lo - ROW3
                else:
                    src, st = xsh[(who, k // 4, i // 2)], lo - ROW3 * i
                return src[:, st : st + F * NB].rearrange("p (a c) -> p a c", c=F)[:, a0 : a0 + na, 0:ln]

            def mult(who, job):
                k, a0, na = job
                q = k % 4
                if who == "v":
                    eng = nc.vector
                    pd = prod_pool.tile([P, NB, QF], F32, name="pd", tag="pd", align_bytes=64)
                    wk = wps[k][:, a0 : a0 + na]
                else:
                    eng = nc.gpsimd
                    pd = gm_pool.tile([P, NB, QF], F32, name="gm", tag="gm")
                    wk = wsb[k][:, a0 : a0 + na]
                prod[job] = pd
                for lo, hi, whole in pieces(q):
                    ln = hi - lo
                    win = source(who, job, lo, ln)
                    dst = pd[:, 0:na, lo - QF * q : hi - QF * q]
                    w0 = TAPS * blocks(q).index((lo // GRP, lo // ROW3))
                    if whole:
                        eng.tensor_tensor(
                            out=dst.rearrange("p a (j m) -> p a j m", m=TAPS),
                            in0=win.rearrange("p a (j m) -> p a j m", m=TAPS),
                            in1=wk[:, :, w0 : w0 + TAPS].unsqueeze(2).to_broadcast([P, na, ln // TAPS, TAPS]),
                            op=MULT,
                        )
                    else:
                        m0 = lo % TAPS
                        eng.tensor_tensor(out=dst, in0=win, in1=wk[:, :, w0 + m0 : w0 + m0 + ln], op=MULT)

            def small_products(job):
                k, a0, na = job
                q = k % 4
                pd = gm_pool.tile([P, TAPS, na, QO], F32, name="sm", tag="sm", bufs=1)
                prod[job] = pd
                steps = []
                for lo, hi, whole in pieces(q):
                    w0 = TAPS * blocks(q).index((lo // GRP, lo // ROW3))
                    win = source("g", job, lo, hi - lo)
                    o0 = (lo - QF * q) // TAPS
                    for a in range(na):
                        for m in range(TAPS):
                            steps.append(
                                (
                                    pd[:, m, a, o0 : o0 + (hi - lo) // TAPS],
                                    win[:, a, m : hi - lo : TAPS],
                                    wsb[k][:, a0 + a, w0 + m : w0 + m + 1],
                                )
                            )
                return steps

            def store(queue, job, a, na, t):
                k = job[0]
                n, q = k // 4, k % 4
                v0 = NB * n + job[1] + a
                queue.dma_start(out=out_v[:, v0 : v0 + na, QO * q : QO * (q + 1)], in_=t[:, 0:na, :])

            def tap(job, r, m):
                if job == S_JOB:
                    n = job[2] * QO
                    return prod[job][:].rearrange("p m a o -> p (m a o)")[:, n * m + P * r : n * m + P * (r + 1)]
                f0 = 2 * QF * r + m
                return prod[job][:].rearrange("p a f -> p (a f)")[:, f0 : f0 + TAPS * (P - 1) + 1 : TAPS]

            def tapsum_pe(job, last):
                npair = job[2] // 2
                acc = ps_a.tile([P, NB // 2, P], F32, name="acc", tag="a")
                for r in range(npair):
                    for m in range(TAPS):
                        nc.tensor.matmul(
                            out=acc[:, r, :],
                            lhsT=tap(job, r, m),
                            rhs=ident[:],
                            is_transpose=True,
                            start=(m == 0),
                            stop=(m == TAPS - 1),
                        )
                    if r == 0 and last is not None:
                        back(last)
                t = ot_pool.tile([P, NB // 2, P], F32, name="o_t", tag="o_t")
                nc.scalar.copy(out=t[:, 0:npair, :], in_=acc[:, 0:npair, :])
                o_t[job] = t

            def back(job):
                npair = job[2] // 2
                ob = ps_b.tile([P, NB // 2, P], F32, name="ob", tag="b")
                for r in range(npair):
                    nc.tensor.transpose(ob[:, r, :], o_t[job][:, r, :], ident[:])
                t = osb_pool.tile([P, NB, QO], F32, name="osb", tag="osb")
                nc.scalar.copy(
                    out=t[:, 0 : job[2], :].rearrange("p a o -> p (a o)"),
                    in_=ob[:, 0:npair, :].rearrange("p r c -> p (r c)"),
                )
                store(nc.scalar, job, 0, job[2], t)

            def tapsum_v(job, cuts):
                pv = prod[job][:].rearrange("p a (o m) -> p a o m", m=TAPS)
                a = 0
                for n in cuts:
                    t = osb_pool.tile([P, NB, OV], F32, name="osv", tag="osv")
                    nc.vector.tensor_reduce(
                        out=t[:, 0:n, 0:QO], in_=pv[:, a : a + n], axis=mybir.AxisListType.X, op=ADD
                    )
                    store(nc.sync, job, a, n, t[:, :, 0:QO])
                    a += n

            ph2.enter_context(
                tc.manual_schedule(
                    engines={mybir.EngineType.PE, mybir.EngineType.DVE, mybir.EngineType.Activation, mybir.EngineType.SP}
                )
            )
            jobs = {"v": V_JOBS, "g": G_JOBS, "s": (S_JOB,)}
            sums = [jobs[who][i] for who, i in PE_ORDER]
            small = small_products(S_JOB)
            share = -(-len(small) // S_PART)
            done = []
            for job in G_JOBS[0:G_BUFS]:
                mult("g", job)
            for i in range(len(V_JOBS)):
                job = V_JOBS[i]
                mult("v", job)
                if i + 2 < len(V_JOBS):
                    rows("v", V_JOBS[i + 2][0])
                    wcopy(V_JOBS[i + 2][0])
                if i in V_SUM:
                    tapsum_v(job, (3, 3, 1, 1) if i == len(V_JOBS) - 1 else (5, 3))
                while sums and sums[0] in prod:
                    job = sums.pop(0)
                    while job == S_JOB and small:
                        dst, src, w = small.pop(0)
                        nc.scalar.activation(out=dst, in_=src, func=ACT.Copy, scale=w)
                    tapsum_pe(job, done[-1] if done else None)
                    done.append(job)
                    for n in range(share):
                        if small:
                            dst, src, w = small.pop(0)
                            nc.scalar.activation(out=dst, in_=src, func=ACT.Copy, scale=w)
                    if job in G_JOBS and G_JOBS.index(job) + G_BUFS < len(G_JOBS):
                        nxt = G_JOBS[G_JOBS.index(job) + G_BUFS]
                        rows("g", nxt[0])
                        mult("g", nxt)
                    if sums and sums[0] in G_JOBS and i + 1 < len(V_JOBS):
                        break
            back(done[-1])
